import numpy as np
import ml_dtypes


def mxq(x, axis, fmt="e4m3"):
    dtype, down = {"e4m3": (ml_dtypes.float8_e4m3fn, 7), "e5m2": (ml_dtypes.float8_e5m2, 14)}[fmt]
    v = np.moveaxis(np.asarray(x, np.float32).astype(ml_dtypes.bfloat16).astype(np.float64), axis, -1)
    blocks = v.reshape(v.shape[:-1] + (-1, 32))
    amax = np.abs(blocks).max(-1, keepdims=True)
    byte = np.maximum(np.where(amax > 0, np.frexp(amax)[1] - 1 + 127, 0) - down, 1)
    scale = np.exp2(byte - 127.0)
    codes = (blocks / scale).astype(np.float32).astype(dtype).astype(np.float64)
    return np.moveaxis((codes * scale).reshape(v.shape), -1, axis)


WIDE = False


def mx_kscale(k):
    if not WIDE:
        return np.ones(k)
    levels = np.array([10, -10, 5, -5, 0])
    a = np.random.permutation(np.resize(levels, k // 512 * 4)).reshape(k // 512, 4)
    idx = np.arange(k)
    return np.exp2(a[idx // 512, idx % 128 // 32])


BF16 = ml_dtypes.bfloat16


def bf(x):
    return np.asarray(x, np.float32).astype(BF16)


def f64(x):
    return np.asarray(x).astype(np.float64)


E2M1 = np.array([0.0, 0.5, 1.0, 1.5, 2.0, 3.0, 4.0, 6.0, -0.0, -0.5, -1.0, -1.5, -2.0, -3.0, -4.0, -6.0])


def pack_weight(w, fmt):
    k, n = w.shape
    w = f64(bf(w)).reshape(k // 32, 32, n)
    amax = np.abs(w).max(1)
    if fmt == "e4m3":
        byte = np.frexp(amax)[1] - 1 + 127 - 7
    else:
        mant, ex = np.frexp(amax / 6.0)
        byte = np.where(mant > 0.5, ex, ex - 1) + 127
    byte = np.clip(np.where(amax > 0, byte, 1), 1, 254)
    scaled = (w * np.exp2(127.0 - byte)[:, None, :]).reshape(k, n).astype(np.float32)
    by_word = np.ascontiguousarray(scaled.reshape(k // 512, 128, 4, n).transpose(0, 1, 3, 2))
    if fmt == "e4m3":
        words = by_word.astype(ml_dtypes.float8_e4m3fn).view(np.uint8)
    else:
        c = by_word.astype(ml_dtypes.float4_e2m1fn).view(np.uint8) & 0xF
        words = c[..., 0::2] | (c[..., 1::2] << 4)
    return np.ascontiguousarray(words), np.ascontiguousarray(byte.astype(np.uint8).reshape(k // 512, 16, n))


def unpack_weight(words, scales, fmt):
    g, p, n, _ = words.shape
    if fmt == "e4m3":
        vals = np.ascontiguousarray(words).view(ml_dtypes.float8_e4m3fn).astype(np.float64)
    else:
        nib = np.empty((g, p, n, 4), np.uint8)
        nib[..., 0::2] = words & 0xF
        nib[..., 1::2] = words >> 4
        vals = E2M1[nib]
    vals = vals * np.repeat(np.exp2(scales.astype(np.float64) - 127.0), 8, axis=1)[..., None]
    return vals.transpose(0, 1, 3, 2).reshape(g * 512, n)


B, S, D, E = 2, 512, 1024, 1024
INV_SQRT2 = 0.7071067811865476
FMT = "e4m3"


def dwt_haar(x):
    e = x[..., 0::2]
    o = x[..., 1::2]
    return (e + o) * INV_SQRT2, (o - e) * INV_SQRT2


def idwt_haar(L, H):
    a = (L - H) * INV_SQRT2
    b = (L + H) * INV_SQRT2
    return np.stack([a, b], axis=-1).reshape(*L.shape[:-1], -1)


def softmax(v):
    p = np.exp(v - v.max(-1, keepdims=True))
    return p / p.sum(-1, keepdims=True)


def setup_inputs():
    s = mx_kscale(D)
    x = bf(np.random.standard_normal((B, S, D)) * s)
    W_q_words, W_q_scales = pack_weight(np.ascontiguousarray((np.random.standard_normal((E, D)) * 1.5 / np.sqrt(D) / s).T), FMT)
    b_q = bf(np.random.standard_normal(E) * 0.5)
    W_k_words, W_k_scales = pack_weight(np.ascontiguousarray((np.random.standard_normal((E, D)) * 1.5 / np.sqrt(D) / s).T), FMT)
    b_k = bf(np.random.standard_normal(E) * 0.5)
    W_v_words, W_v_scales = pack_weight(np.ascontiguousarray((np.random.standard_normal((E, D)) * 2.0 / np.sqrt(D) / s).T), FMT)
    b_v = bf(np.random.standard_normal(E) * 0.5)
    return {"x": x,
            "W_q_words": W_q_words, "W_q_scales": W_q_scales,
            "b_q": b_q,
            "W_k_words": W_k_words, "W_k_scales": W_k_scales,
            "b_k": b_k,
            "W_v_words": W_v_words, "W_v_scales": W_v_scales,
            "b_v": b_v}


def reference(x, W_q_words, W_q_scales, b_q, W_k_words, W_k_scales, b_k, W_v_words, W_v_scales, b_v):
    nb, ns = x.shape[0], x.shape[1]
    xq = mxq(f64(x), 2, "e4m3")
    q = (xq @ unpack_weight(W_q_words, W_q_scales, FMT)) + f64(b_q)
    k = (xq @ unpack_weight(W_k_words, W_k_scales, FMT)) + f64(b_k)
    v = (xq @ unpack_weight(W_v_words, W_v_scales, FMT)) + f64(b_v)
    q_L, q_H = dwt_haar(q)
    k_L, k_H = dwt_haar(k)
    v_L, v_H = dwt_haar(v)
    L = softmax(q_L + k_L)
    H = softmax(q_H + k_H)
    L_out = softmax(L + v_L)
    H_out = softmax(H + v_H)
    out = idwt_haar(L_out, H_out)
    return out.reshape(nb, ns, -1)

@@ -1,0 +1,282 @@
+from contextlib import ExitStack
+
+import concourse.mybir as mybir
+from concourse.masks import make_identity
+
+F32 = mybir.dt.float32
+BF16 = mybir.dt.bfloat16
+I32 = mybir.dt.int32
+U32 = mybir.dt.uint32
+U8 = mybir.dt.uint8
+FP8X4 = mybir.dt.float8_e4m3fn_x4
+ALU = mybir.AluOpType
+ACT = mybir.ActivationFunctionType
+AXIS = mybir.AxisListType
+
+P = 128
+TOKENS = 1024
+D = 1024
+E = 1024
+N_TILES = TOKENS // P
+K_PASS = 512
+GROUPS = D // K_PASS
+BANK = 512
+BANKS = E // BANK
+PAIRS = E // 2
+BANK_PAIRS = BANK // 2
+INV_SQRT2 = 0.7071067811865476
+
+FLOPS = 3 * 2 * TOKENS * D * E
+
+
+def tile_waveletmultiheadattention_kernel(
+    tc, x, W_q_words, W_q_scales, b_q, W_k_words, W_k_scales, b_k, W_v_words, W_v_scales, b_v, out
+):
+    nc = tc.nc
+    x_rows = x.flatten_outer_dims()
+    out_rows = out.flatten_outer_dims()
+    words_in = (W_q_words, W_k_words, W_v_words)
+    scales_in = (W_q_scales, W_k_scales, W_v_scales)
+    biases_in = (b_q, b_k, b_v)
+    sums = ((0, 1), (2,))
+
+    with ExitStack() as ctx:
+        keep = ctx.enter_context(tc.tile_pool(name="keep", bufs=1))
+        work = ctx.enter_context(tc.tile_pool(name="work", bufs=3))
+        stats = ctx.enter_context(tc.tile_pool(name="stats", bufs=4))
+        psum_qk = ctx.enter_context(tc.psum_pool(name="psum_qk", bufs=2))
+        psum_v = ctx.enter_context(tc.psum_pool(name="psum_v", bufs=1))
+        psum_aux = ctx.enter_context(tc.psum_pool(name="psum_aux", bufs=2))
+        psum_of_sum = (psum_qk, psum_v)
+
+        x_sb = keep.tile([P, N_TILES, D], BF16)
+        x_codes = keep.tile([P, N_TILES, GROUPS * P], U32, align_bytes=64)
+        x_planes = keep.tile([P, N_TILES, GROUPS * P], U8, align_bytes=64)
+        w_words = keep.tile([P, 3, GROUPS, E], U32, align_bytes=64)
+        w_planes = keep.tile([P, 3, E], U8, align_bytes=64)
+        bias_rows = keep.tile([P, 3, E], BF16)
+        beta = keep.tile([P, 2, 2, PAIRS], F32)
+        ident = keep.tile([P, P], F32)
+        ones = keep.tile([P, P], BF16)
+        signs = keep.tile([P, 2, 2], F32)
+        warm = keep.tile([P, 1], F32)
+
+        nc.vector.memset(bias_rows[:].rearrange("p w n -> p (w n)").bitcast(I32), 0)
+        nc.vector.memset(w_planes[:].rearrange("p w n -> p (w n)").bitcast(I32), 0)
+        nc.vector.memset(ones[:], 1.0)
+        nc.vector.memset(signs[:], 1.0)
+        nc.vector.memset(signs[:, 1, 0:1], -1.0)
+        make_identity(nc, ident[:])
+        nc.scalar.activation(out=warm[:], in_=signs[:, 0, 0:1], func=ACT.Exp)
+
+        def load_x(i):
+            nc.sync.dma_start(out=x_sb[:, i, :], in_=x_rows[i * P : (i + 1) * P, :])
+
+        def load_words(w, h):
+            src = words_in[w].rearrange("g p n t -> p g (n t)")
+            nc.sync.dma_start(
+                out=w_words[:, w, :, h * BANK : (h + 1) * BANK].bitcast(I32),
+                in_=src[:, :, 4 * h * BANK : 4 * (h + 1) * BANK].bitcast(I32),
+            )
+
+        def load_planes(w):
+            for c in range(4):
+                nc.sync.dma_start(
+                    out=w_planes[32 * c : 32 * c + 4 * GROUPS, w, :].bitcast(I32),
+                    in_=scales_in[w][:, 4 * c : 4 * c + 4, :].bitcast(I32),
+                )
+
+        for w in range(3):
+            nc.scalar.dma_start(
+                out=bias_rows[0:1, w, :], in_=biases_in[w].rearrange("(o n) -> o n", o=1)
+            )
+        load_x(0)
+        load_words(0, 0)
+        load_words(1, 0)
+        load_planes(0)
+        load_planes(1)
+        load_words(0, 1)
+        load_words(1, 1)
+        load_x(1)
+        load_planes(2)
+        load_words(2, 0)
+        load_words(2, 1)
+        for i in range(2, N_TILES):
+            load_x(i)
+
+        held = {}
+
+        def spread_biases():
+            for s in range(2):
+                for h in range(BANKS):
+                    spread = psum_aux.tile([P, BANK], F32, tag="aux")
+                    for n, w in enumerate(sums[s]):
+                        nc.tensor.matmul(
+                            out=spread[:],
+                            lhsT=ones[:],
+                            rhs=bias_rows[:, w, h * BANK : (h + 1) * BANK],
+                            start=(n == 0),
+                            stop=(n == len(sums[s]) - 1),
+                        )
+                    nc.scalar.activation(
+                        out=beta[:, s, :, h * BANK_PAIRS : (h + 1) * BANK_PAIRS],
+                        in_=spread[:].rearrange("p (j t) -> p t j", t=2),
+                        func=ACT.Copy,
+                        scale=INV_SQRT2,
+                    )
+
+        def quantise_x(i):
+            x_words = x_sb[:, i, :].bitcast(F32)
+            turned = psum_aux.tile([P, BANK], F32, tag="aux")
+            for g in range(GROUPS):
+                for u in range(2):
+                    nc.tensor.transpose(
+                        turned[:, (2 * g + u) * P : (2 * g + u + 1) * P],
+                        x_words[:, 256 * g + u : 256 * (g + 1) : 2],
+                        ident[:],
+                    )
+            grouped = work.tile([P, GROUPS * P * 4], BF16, align_bytes=64, tag="grouped")
+            nc.scalar.copy(
+                out=grouped[:].bitcast(F32).rearrange("p (g r u) -> p g r u", g=GROUPS, u=2),
+                in_=turned[:].rearrange("p (g u r) -> p g r u", g=GROUPS, u=2),
+            )
+            nc.vector.quantize_mx(
+                out=x_codes[:, i, :].bitcast(FP8X4), scales=x_planes[:, i, :], in_=grouped[:]
+            )
+
+        def project(i):
+            for s in range(2):
+                passes = [(w, g) for w in sums[s] for g in range(GROUPS)]
+                for h in range(BANKS):
+                    acc = psum_of_sum[s].tile([P, BANK], F32, tag="acc%d%d" % (s, h))
+                    for n, (w, g) in enumerate(passes):
+                        nc.tensor.matmul_mx(
+                            out=acc[:],
+                            lhsT=x_codes[:, i, g * P : (g + 1) * P].bitcast(FP8X4),
+                            lhsT_scale=x_planes[:, i, g * P : (g + 1) * P],
+                            rhs=w_words[:, w, g, h * BANK : (h + 1) * BANK].bitcast(FP8X4),
+                            rhs_scale=w_planes[4 * g : P, w, h * BANK : (h + 1) * BANK],
+                            start=(n == 0),
+                            stop=(n == len(passes) - 1),
+                        )
+                    held["acc", s, h, i] = acc
+
+        def add_bias(i):
+            for s in range(2):
+                biased = work.tile([P, 2, PAIRS], F32, tag="biased%d" % s)
+                for h in range(BANKS):
+                    cols = slice(h * BANK_PAIRS, (h + 1) * BANK_PAIRS)
+                    nc.vector.scalar_tensor_tensor(
+                        out=biased[:, :, cols],
+                        in0=held["acc", s, h, i][:].rearrange("p (j t) -> p t j", t=2),
+                        scalar=INV_SQRT2,
+                        in1=beta[:, s, :, cols],
+                        op0=ALU.mult,
+                        op1=ALU.add,
+                    )
+                held["biased", s, i] = biased
+
+        def haar(i):
+            for s in range(2):
+                biased = held["biased", s, i]
+                bands = work.tile([P, 2, PAIRS], F32, tag="bands%d" % s)
+                nc.gpsimd.tensor_tensor(
+                    out=bands[:, 0, :], in0=biased[:, 0, :], in1=biased[:, 1, :], op=ALU.add
+                )
+                nc.gpsimd.tensor_tensor(
+                    out=bands[:, 1, :], in0=biased[:, 1, :], in1=biased[:, 0, :], op=ALU.subtract
+                )
+                held["bands", s, i] = bands
+
+        def exp_shifted(logits, stage, i):
+            neg_max = stats.tile([P, 2], F32, tag="neg_max%d" % stage)
+            nc.vector.tensor_reduce(
+                out=neg_max[:], in_=logits[:], axis=AXIS.X, op=ALU.max, negate=True
+            )
+            numer = work.tile([P, 2, PAIRS], F32, tag="numer%d" % stage)
+            total = stats.tile([P, 2], F32, tag="total%d" % stage)
+            for band in range(2):
+                nc.scalar.activation(
+                    out=numer[:, band, :],
+                    in_=logits[:, band, :],
+                    func=ACT.Exp,
+                    bias=neg_max[:, band : band + 1],
+                    scale=1.0,
+                    accum_out=total[:, band : band + 1],
+                )
+            held["numer", stage, i] = numer
+            held["total", stage, i] = total
+
+        def add_v(i):
+            inv = stats.tile([P, 2], F32, tag="inv1")
+            nc.vector.reciprocal(out=inv[:], in_=held["total", 1, i][:])
+            logits2 = work.tile([P, 2, PAIRS], F32, tag="logits2")
+            for band in range(2):
+                nc.vector.scalar_tensor_tensor(
+                    out=logits2[:, band, :],
+                    in0=held["numer", 1, i][:, band, :],
+                    scalar=inv[:, band : band + 1],
+                    in1=held["bands", 1, i][:, band, :],
+                    op0=ALU.mult,
+                    op1=ALU.add,
+                )
+            held["logits2", i] = logits2
+
+        def scale_high(i):
+            inv = stats.tile([P, 2], F32, tag="inv2")
+            nc.vector.reciprocal(out=inv[:], in_=held["total", 2, i][:])
+            gains = stats.tile([P, 2, 2], F32, tag="gains")
+            nc.vector.scalar_tensor_tensor(
+                out=gains[:],
+                in0=inv[:].unsqueeze(2).to_broadcast([P, 2, 2]),
+                scalar=INV_SQRT2,
+                in1=signs[:],
+                op0=ALU.mult,
+                op1=ALU.mult,
+            )
+            high = work.tile([P, 2, PAIRS], F32, tag="high")
+            for t in range(2):
+                nc.scalar.activation(
+                    out=high[:, t, :],
+                    in_=held["numer", 2, i][:, 1, :],
+                    func=ACT.Copy,
+                    scale=gains[:, 1, t : t + 1],
+                )
+            held["gains", i] = gains
+            held["high", i] = high
+
+        def inverse_haar(i):
+            rows = work.tile([P, E], F32, tag="rows")
+            nc.vector.scalar_tensor_tensor(
+                out=rows[:].rearrange("p (j t) -> p j t", t=2),
+                in0=held["numer", 2, i][:, 0, :].unsqueeze(2).to_broadcast([P, PAIRS, 2]),
+                scalar=held["gains", i][:, 0, 0:1],
+                in1=held["high", i][:].rearrange("p t j -> p j t"),
+                op0=ALU.mult,
+                op1=ALU.add,
+            )
+            nc.sync.dma_start(out=out_rows[i * P : (i + 1) * P, :], in_=rows[:])
+
+        def live(i):
+            return 0 <= i < N_TILES
+
+        quantise_x(0)
+        spread_biases()
+        for k in range(-2, N_TILES + 1):
+            if live(k - 1):
+                exp_shifted(held["logits2", k - 1], 2, k - 1)
+            if live(k):
+                exp_shifted(held["bands", 0, k], 1, k)
+            if live(k + 2):
+                project(k + 2)
+                add_bias(k + 2)
+            if live(k - 1):
+                scale_high(k - 1)
+            if live(k + 1):
+                haar(k + 1)
+            if live(k + 3):
+                quantise_x(k + 3)
+            if live(k):
+                add_v(k)
+            if live(k - 1):
+                inverse_haar(k - 1)

@@ -24,6 +24,7 @@ BANK = 512
 BANKS = E // BANK
 PAIRS = E // 2
 BANK_PAIRS = BANK // 2
+X_PAIRS = N_TILES // 2
 INV_SQRT2 = 0.7071067811865476
 
 FLOPS = 3 * 2 * TOKENS * D * E
@@ -38,16 +39,17 @@ def tile_waveletmultiheadattention_kernel(
     words_in = (W_q_words, W_k_words, W_v_words)
     scales_in = (W_q_scales, W_k_scales, W_v_scales)
     biases_in = (b_q, b_k, b_v)
-    sums = ((0, 1), (2,))
+    QK = (0, 1)
+    V = (2,)
 
     with ExitStack() as ctx:
         keep = ctx.enter_context(tc.tile_pool(name="keep", bufs=1))
         work = ctx.enter_context(tc.tile_pool(name="work", bufs=3))
+        whole = ctx.enter_context(tc.tile_pool(name="whole", bufs=N_TILES))
         stats = ctx.enter_context(tc.tile_pool(name="stats", bufs=4))
-        psum_qk = ctx.enter_context(tc.psum_pool(name="psum_qk", bufs=2))
-        psum_v = ctx.enter_context(tc.psum_pool(name="psum_v", bufs=1))
+        psum_acc = ctx.enter_context(tc.psum_pool(name="psum_acc", bufs=3))
         psum_aux = ctx.enter_context(tc.psum_pool(name="psum_aux", bufs=2))
-        psum_of_sum = (psum_qk, psum_v)
+        ctx.enter_context(tc.manual_schedule())
 
         x_sb = keep.tile([P, N_TILES, D], BF16)
         x_codes = keep.tile([P, N_TILES, GROUPS * P], U32, align_bytes=64)
@@ -55,22 +57,25 @@ def tile_waveletmultiheadattention_kernel(
         w_words = keep.tile([P, 3, GROUPS, E], U32, align_bytes=64)
         w_planes = keep.tile([P, 3, E], U8, align_bytes=64)
         bias_rows = keep.tile([P, 3, E], BF16)
-        beta = keep.tile([P, 2, 2, PAIRS], F32)
+        beta_qk = keep.tile([P, 2, PAIRS], F32)
+        beta_v = keep.tile([P, 2, PAIRS], F32)
         ident = keep.tile([P, P], F32)
         ones = keep.tile([P, P], BF16)
-        signs = keep.tile([P, 2, 2], F32)
+        minus_ones = keep.tile([P, P], BF16)
         warm = keep.tile([P, 1], F32)
 
         nc.vector.memset(bias_rows[:].rearrange("p w n -> p (w n)").bitcast(I32), 0)
         nc.vector.memset(w_planes[:].rearrange("p w n -> p (w n)").bitcast(I32), 0)
         nc.vector.memset(ones[:], 1.0)
-        nc.vector.memset(signs[:], 1.0)
-        nc.vector.memset(signs[:, 1, 0:1], -1.0)
+        nc.vector.memset(minus_ones[:], -1.0)
+        nc.vector.memset(warm[:], 0.0)
         make_identity(nc, ident[:])
-        nc.scalar.activation(out=warm[:], in_=signs[:, 0, 0:1], func=ACT.Exp)
 
-        def load_x(i):
-            nc.sync.dma_start(out=x_sb[:, i, :], in_=x_rows[i * P : (i + 1) * P, :])
+        def load_x(pair):
+            nc.sync.dma_start(
+                out=x_sb[:, 2 * pair : 2 * pair + 2, :],
+                in_=x_rows[2 * pair * P : (2 * pair + 2) * P, :].rearrange("(a p) k -> p a k", p=P),
+            )
 
         def load_words(w, h):
             src = words_in[w].rearrange("g p n t -> p g (n t)")
@@ -90,193 +95,244 @@ def tile_waveletmultiheadattention_kernel(
             nc.scalar.dma_start(
                 out=bias_rows[0:1, w, :], in_=biases_in[w].rearrange("(o n) -> o n", o=1)
             )
-        load_x(0)
-        load_words(0, 0)
-        load_words(1, 0)
-        load_planes(0)
-        load_planes(1)
-        load_words(0, 1)
-        load_words(1, 1)
-        load_x(1)
+        nc.scalar.activation(out=warm[:], in_=warm[:], func=ACT.Exp)
+        for pair in range(X_PAIRS):
+            load_x(pair)
+        for h, w_planes_now in enumerate(QK):
+            load_planes(w_planes_now)
+            for w in QK:
+                load_words(w, h)
         load_planes(2)
-        load_words(2, 0)
-        load_words(2, 1)
-        for i in range(2, N_TILES):
-            load_x(i)
+        for h in range(BANKS):
+            load_words(2, h)
 
         held = {}
 
-        def spread_biases():
-            for s in range(2):
-                for h in range(BANKS):
-                    spread = psum_aux.tile([P, BANK], F32, tag="aux")
-                    for n, w in enumerate(sums[s]):
-                        nc.tensor.matmul(
-                            out=spread[:],
-                            lhsT=ones[:],
-                            rhs=bias_rows[:, w, h * BANK : (h + 1) * BANK],
-                            start=(n == 0),
-                            stop=(n == len(sums[s]) - 1),
-                        )
-                    nc.scalar.activation(
-                        out=beta[:, s, :, h * BANK_PAIRS : (h + 1) * BANK_PAIRS],
-                        in_=spread[:].rearrange("p (j t) -> p t j", t=2),
-                        func=ACT.Copy,
-                        scale=INV_SQRT2,
-                    )
+        def spread_bias(plane, terms):
+            spread = psum_aux.tile([P, BANK], F32, tag="aux")
+            for n, (w, t, sign) in enumerate(terms):
+                nc.tensor.matmul(
+                    out=spread[:],
+                    lhsT=sign[:],
+                    rhs=bias_rows[:, w, t:E:2],
+                    start=(n == 0),
+                    stop=(n == len(terms) - 1),
+                )
+            nc.scalar.activation(out=plane, in_=spread[:], func=ACT.Copy, scale=INV_SQRT2)
 
-        def quantise_x(i):
-            x_words = x_sb[:, i, :].bitcast(F32)
-            turned = psum_aux.tile([P, BANK], F32, tag="aux")
-            for g in range(GROUPS):
-                for u in range(2):
-                    nc.tensor.transpose(
-                        turned[:, (2 * g + u) * P : (2 * g + u + 1) * P],
-                        x_words[:, 256 * g + u : 256 * (g + 1) : 2],
-                        ident[:],
-                    )
-            grouped = work.tile([P, GROUPS * P * 4], BF16, align_bytes=64, tag="grouped")
-            nc.scalar.copy(
-                out=grouped[:].bitcast(F32).rearrange("p (g r u) -> p g r u", g=GROUPS, u=2),
-                in_=turned[:].rearrange("p (g u r) -> p g r u", g=GROUPS, u=2),
-            )
+        def turn_x(pair):
+            grouped = work.tile([P, 2, GROUPS * P * 4], BF16, align_bytes=64, tag="grouped", bufs=2)
+            for a in range(2):
+                x_words = x_sb[:, 2 * pair + a, :].bitcast(F32)
+                turned = psum_acc.tile([P, BANK], F32, tag="acc%d" % a)
+                for g in range(GROUPS):
+                    for u in range(2):
+                        nc.tensor.transpose(
+                            turned[:, (2 * g + u) * P : (2 * g + u + 1) * P],
+                            x_words[:, 256 * g + u : 256 * (g + 1) : 2],
+                            ident[:],
+                        )
+                copy = (nc.scalar.copy, nc.vector.tensor_copy)[a]
+                copy(
+                    out=grouped[:, a, :].bitcast(F32).rearrange("p (g r u) -> p g r u", g=GROUPS, u=2),
+                    in_=turned[:].rearrange("p (g u r) -> p g r u", g=GROUPS, u=2),
+                )
+            held["grouped", pair] = grouped
+
+        def quantise_x(pair):
             nc.vector.quantize_mx(
-                out=x_codes[:, i, :].bitcast(FP8X4), scales=x_planes[:, i, :], in_=grouped[:]
+                out=x_codes[:, 2 * pair : 2 * pair + 2, :].rearrange("p a c -> p (a c)").bitcast(FP8X4),
+                scales=x_planes[:, 2 * pair : 2 * pair + 2, :].rearrange("p a c -> p (a c)"),
+                in_=held["grouped", pair][:].rearrange("p a c -> p (a c)"),
             )
 
-        def project(i):
-            for s in range(2):
-                passes = [(w, g) for w in sums[s] for g in range(GROUPS)]
-                for h in range(BANKS):
-                    acc = psum_of_sum[s].tile([P, BANK], F32, tag="acc%d%d" % (s, h))
-                    for n, (w, g) in enumerate(passes):
-                        nc.tensor.matmul_mx(
-                            out=acc[:],
-                            lhsT=x_codes[:, i, g * P : (g + 1) * P].bitcast(FP8X4),
-                            lhsT_scale=x_planes[:, i, g * P : (g + 1) * P],
-                            rhs=w_words[:, w, g, h * BANK : (h + 1) * BANK].bitcast(FP8X4),
-                            rhs_scale=w_planes[4 * g : P, w, h * BANK : (h + 1) * BANK],
-                            start=(n == 0),
-                            stop=(n == len(passes) - 1),
-                        )
-                    held["acc", s, h, i] = acc
-
-        def add_bias(i):
-            for s in range(2):
-                biased = work.tile([P, 2, PAIRS], F32, tag="biased%d" % s)
-                for h in range(BANKS):
-                    cols = slice(h * BANK_PAIRS, (h + 1) * BANK_PAIRS)
-                    nc.vector.scalar_tensor_tensor(
-                        out=biased[:, :, cols],
-                        in0=held["acc", s, h, i][:].rearrange("p (j t) -> p t j", t=2),
-                        scalar=INV_SQRT2,
-                        in1=beta[:, s, :, cols],
-                        op0=ALU.mult,
-                        op1=ALU.add,
+        def project(i, name, weights):
+            passes = [(w, g) for w in weights for g in range(GROUPS)]
+            for h in range(BANKS):
+                acc = psum_acc.tile([P, BANK], F32, tag="acc%d" % h)
+                for n, (w, g) in enumerate(passes):
+                    nc.tensor.matmul_mx(
+                        out=acc[:],
+                        lhsT=x_codes[:, i, g * P : (g + 1) * P].bitcast(FP8X4),
+                        lhsT_scale=x_planes[:, i, g * P : (g + 1) * P],
+                        rhs=w_words[:, w, g, h * BANK : (h + 1) * BANK].bitcast(FP8X4),
+                        rhs_scale=w_planes[4 * g : P, w, h * BANK : (h + 1) * BANK],
+                        start=(n == 0),
+                        stop=(n == len(passes) - 1),
                     )
-                held["biased", s, i] = biased
+                held[name, h, i] = acc
 
-        def haar(i):
-            for s in range(2):
-                biased = held["biased", s, i]
-                bands = work.tile([P, 2, PAIRS], F32, tag="bands%d" % s)
-                nc.gpsimd.tensor_tensor(
-                    out=bands[:, 0, :], in0=biased[:, 0, :], in1=biased[:, 1, :], op=ALU.add
-                )
-                nc.gpsimd.tensor_tensor(
-                    out=bands[:, 1, :], in0=biased[:, 1, :], in1=biased[:, 0, :], op=ALU.subtract
-                )
-                held["bands", s, i] = bands
+        def parity(acc, t):
+            one = acc[:].rearrange("p (j t) -> p t j", t=2)[:, t, :]
+            return one.unsqueeze(1).to_broadcast([P, 2, BANK_PAIRS])
 
-        def exp_shifted(logits, stage, i):
-            neg_max = stats.tile([P, 2], F32, tag="neg_max%d" % stage)
-            nc.vector.tensor_reduce(
-                out=neg_max[:], in_=logits[:], axis=AXIS.X, op=ALU.max, negate=True
+        def qk_out_of_psum(i):
+            biased = work.tile([P, 2, PAIRS], F32, tag="biased")
+            for h in range(BANKS):
+                cols = slice(h * BANK_PAIRS, (h + 1) * BANK_PAIRS)
+                nc.vector.scalar_tensor_tensor(
+                    out=biased[:, :, cols],
+                    in0=held["qk", h, i][:].rearrange("p (j t) -> p t j", t=2),
+                    scalar=INV_SQRT2,
+                    in1=beta_qk[:, :, cols],
+                    op0=ALU.mult,
+                    op1=ALU.add,
+                )
+            held["biased", i] = biased
+
+        def qk_haar(i):
+            biased = held["biased", i]
+            bands = whole.tile([P, 2, PAIRS], F32, tag="bands")
+            nc.gpsimd.tensor_tensor(
+                out=bands[:, 0, :], in0=biased[:, 0, :], in1=biased[:, 1, :], op=ALU.add
             )
-            numer = work.tile([P, 2, PAIRS], F32, tag="numer%d" % stage)
-            total = stats.tile([P, 2], F32, tag="total%d" % stage)
+            nc.gpsimd.tensor_tensor(
+                out=bands[:, 1, :], in0=biased[:, 1, :], in1=biased[:, 0, :], op=ALU.subtract
+            )
+            held["bands", i] = bands
+
+        def exp_shifted(stage, i):
+            bands = held["bands", i]
+            neg_max = stats.tile([P, 2], F32, tag="neg_max")
+            nc.vector.tensor_reduce(
+                out=neg_max[:], in_=bands[:], axis=AXIS.X, op=ALU.max, negate=True
+            )
+            total = stats.tile([P, 2], F32, tag="total")
             for band in range(2):
                 nc.scalar.activation(
-                    out=numer[:, band, :],
-                    in_=logits[:, band, :],
+                    out=bands[:, band, :],
+                    in_=bands[:, band, :],
                     func=ACT.Exp,
                     bias=neg_max[:, band : band + 1],
                     scale=1.0,
                     accum_out=total[:, band : band + 1],
                 )
-            held["numer", stage, i] = numer
             held["total", stage, i] = total
 
-        def add_v(i):
-            inv = stats.tile([P, 2], F32, tag="inv1")
+        def live(i):
+            return 0 <= i < N_TILES
+
+        def finish_first(i):
+            if not live(i):
+                return
+            inv = stats.tile([P, 2], F32, tag="inv")
             nc.vector.reciprocal(out=inv[:], in_=held["total", 1, i][:])
-            logits2 = work.tile([P, 2, PAIRS], F32, tag="logits2")
+            bands = held["bands", i]
             for band in range(2):
+                nc.scalar.activation(
+                    out=bands[:, band, :],
+                    in_=bands[:, band, :],
+                    func=ACT.Copy,
+                    scale=inv[:, band : band + 1],
+                )
+
+        def v_even(i):
+            part = work.tile([P, 2, PAIRS], F32, tag="part")
+            for h in range(BANKS):
+                cols = slice(h * BANK_PAIRS, (h + 1) * BANK_PAIRS)
                 nc.vector.scalar_tensor_tensor(
-                    out=logits2[:, band, :],
-                    in0=held["numer", 1, i][:, band, :],
-                    scalar=inv[:, band : band + 1],
-                    in1=held["bands", 1, i][:, band, :],
+                    out=part[:, :, cols],
+                    in0=parity(held["v", h, i], 0),
+                    scalar=INV_SQRT2,
+                    in1=beta_v[:, :, cols],
                     op0=ALU.mult,
                     op1=ALU.add,
                 )
-            held["logits2", i] = logits2
+            held["part", i] = part
 
-        def scale_high(i):
-            inv = stats.tile([P, 2], F32, tag="inv2")
+        def add_part(i):
+            bands = held["bands", i]
+            for band, op in enumerate((ALU.add, ALU.subtract)):
+                nc.gpsimd.tensor_tensor(
+                    out=bands[:, band, :],
+                    in0=bands[:, band, :],
+                    in1=held["part", i][:, band, :],
+                    op=op,
+                )
+
+        def v_odd(i):
+            bands = held["bands", i]
+            for h in range(BANKS):
+                cols = slice(h * BANK_PAIRS, (h + 1) * BANK_PAIRS)
+                nc.vector.scalar_tensor_tensor(
+                    out=bands[:, :, cols],
+                    in0=parity(held["v", h, i], 1),
+                    scalar=INV_SQRT2,
+                    in1=bands[:, :, cols],
+                    op0=ALU.mult,
+                    op1=ALU.add,
+                )
+
+        def finish_second(i):
+            if not live(i):
+                return
+            inv = stats.tile([P, 2], F32, tag="inv")
             nc.vector.reciprocal(out=inv[:], in_=held["total", 2, i][:])
-            gains = stats.tile([P, 2, 2], F32, tag="gains")
-            nc.vector.scalar_tensor_tensor(
-                out=gains[:],
-                in0=inv[:].unsqueeze(2).to_broadcast([P, 2, 2]),
-                scalar=INV_SQRT2,
-                in1=signs[:],
-                op0=ALU.mult,
-                op1=ALU.mult,
-            )
-            high = work.tile([P, 2, PAIRS], F32, tag="high")
-            for t in range(2):
+            gains = whole.tile([P, 2], F32, tag="gains")
+            nc.scalar.activation(out=gains[:], in_=inv[:], func=ACT.Copy, scale=INV_SQRT2)
+            minus = stats.tile([P, 1], F32, tag="minus")
+            nc.scalar.activation(out=minus[:], in_=inv[:, 1:2], func=ACT.Copy, scale=-INV_SQRT2)
+            high = whole.tile([P, 2, PAIRS], F32, tag="high")
+            for t, gain in enumerate((minus[:], gains[:, 1:2])):
                 nc.scalar.activation(
-                    out=high[:, t, :],
-                    in_=held["numer", 2, i][:, 1, :],
-                    func=ACT.Copy,
-                    scale=gains[:, 1, t : t + 1],
+                    out=high[:, t, :], in_=held["bands", i][:, 1, :], func=ACT.Copy, scale=gain
                 )
             held["gains", i] = gains
             held["high", i] = high
 
         def inverse_haar(i):
-            rows = work.tile([P, E], F32, tag="rows")
+            rows = whole.tile([P, E], F32, tag="rows")
             nc.vector.scalar_tensor_tensor(
                 out=rows[:].rearrange("p (j t) -> p j t", t=2),
-                in0=held["numer", 2, i][:, 0, :].unsqueeze(2).to_broadcast([P, PAIRS, 2]),
-                scalar=held["gains", i][:, 0, 0:1],
+                in0=held["bands", i][:, 0, :].unsqueeze(2).to_broadcast([P, PAIRS, 2]),
+                scalar=held["gains", i][:, 0:1],
                 in1=held["high", i][:].rearrange("p t j -> p j t"),
                 op0=ALU.mult,
                 op1=ALU.add,
             )
             nc.sync.dma_start(out=out_rows[i * P : (i + 1) * P, :], in_=rows[:])
 
-        def live(i):
-            return 0 <= i < N_TILES
+        def product(n):
+            if n < N_TILES:
+                project(n, "qk", QK)
+            elif n < 2 * N_TILES:
+                project(n - N_TILES, "v", V)
 
-        quantise_x(0)
-        spread_biases()
-        for k in range(-2, N_TILES + 1):
-            if live(k - 1):
-                exp_shifted(held["logits2", k - 1], 2, k - 1)
-            if live(k):
-                exp_shifted(held["bands", 0, k], 1, k)
-            if live(k + 2):
-                project(k + 2)
-                add_bias(k + 2)
-            if live(k - 1):
-                scale_high(k - 1)
-            if live(k + 1):
-                haar(k + 1)
-            if live(k + 3):
-                quantise_x(k + 3)
-            if live(k):
-                add_v(k)
-            if live(k - 1):
-                inverse_haar(k - 1)
+        def first_read(n):
+            if n < N_TILES:
+                qk_out_of_psum(n)
+                qk_haar(n)
+            elif n < 2 * N_TILES:
+                v_even(n - N_TILES)
+                add_part(n - N_TILES)
+
+        for pair in range(X_PAIRS):
+            turn_x(pair)
+            quantise_x(pair)
+            if pair == 0:
+                for t in range(2):
+                    spread_bias(beta_qk[:, t, :], [(w, t, ones) for w in QK])
+        for n in range(2):
+            product(n)
+            first_read(n)
+        product(2)
+        spread_bias(beta_v[:, 0, :], [(2, 0, ones), (2, 1, ones)])
+        spread_bias(beta_v[:, 1, :], [(2, 0, ones), (2, 1, minus_ones)])
+
+        for s in range(N_TILES):
+            exp_shifted(1, s)
+            product(s + 3)
+            first_read(s + 2)
+            finish_first(s - 1)
+
+        for s in range(N_TILES):
+            finish_first(s + N_TILES - 1)
+            v_odd(s)
+            exp_shifted(2, s)
+            product(N_TILES + s + 3)
+            first_read(N_TILES + s + 2)
+            finish_second(s - 1)
+
+        for s in range(N_TILES):
+            inverse_haar(s)
+            finish_second(s + N_TILES - 1)

@@ -34,8 +34,8 @@ def tile_waveletmultiheadattention_kernel(
     tc, x, W_q_words, W_q_scales, b_q, W_k_words, W_k_scales, b_k, W_v_words, W_v_scales, b_v, out
 ):
     nc = tc.nc
-    x_rows = x.flatten_outer_dims()
-    out_rows = out.flatten_outer_dims()
+    x_tiles = x.flatten_outer_dims().rearrange("(p i) k -> p i k", i=N_TILES)
+    out_tiles = out.flatten_outer_dims().rearrange("(p i) n -> p i n", i=N_TILES)
     words_in = (W_q_words, W_k_words, W_v_words)
     scales_in = (W_q_scales, W_k_scales, W_v_scales)
     biases_in = (b_q, b_k, b_v)
@@ -47,8 +47,7 @@ def tile_waveletmultiheadattention_kernel(
         work = ctx.enter_context(tc.tile_pool(name="work", bufs=3))
         whole = ctx.enter_context(tc.tile_pool(name="whole", bufs=N_TILES))
         stats = ctx.enter_context(tc.tile_pool(name="stats", bufs=4))
-        psum_acc = ctx.enter_context(tc.psum_pool(name="psum_acc", bufs=3))
-        psum_aux = ctx.enter_context(tc.psum_pool(name="psum_aux", bufs=2))
+        psum_acc = ctx.enter_context(tc.psum_pool(name="psum_acc", bufs=4))
         ctx.enter_context(tc.manual_schedule())
 
         x_sb = keep.tile([P, N_TILES, D], BF16)
@@ -73,8 +72,7 @@ def tile_waveletmultiheadattention_kernel(
 
         def load_x(pair):
             nc.sync.dma_start(
-                out=x_sb[:, 2 * pair : 2 * pair + 2, :],
-                in_=x_rows[2 * pair * P : (2 * pair + 2) * P, :].rearrange("(a p) k -> p a k", p=P),
+                out=x_sb[:, 2 * pair : 2 * pair + 2, :], in_=x_tiles[:, 2 * pair : 2 * pair + 2, :]
             )
 
         def load_words(w, h):
@@ -108,8 +106,8 @@ def tile_waveletmultiheadattention_kernel(
 
         held = {}
 
-        def spread_bias(plane, terms):
-            spread = psum_aux.tile([P, BANK], F32, tag="aux")
+        def spread_bias(plane, terms, h):
+            spread = psum_acc.tile([P, BANK], F32, tag="acc%d" % h)
             for n, (w, t, sign) in enumerate(terms):
                 nc.tensor.matmul(
                     out=spread[:],
@@ -290,7 +288,7 @@ def tile_waveletmultiheadattention_kernel(
                 op0=ALU.mult,
                 op1=ALU.add,
             )
-            nc.sync.dma_start(out=out_rows[i * P : (i + 1) * P, :], in_=rows[:])
+            nc.sync.dma_start(out=out_tiles[:, i, :], in_=rows[:])
 
         def product(n):
             if n < N_TILES:
@@ -311,28 +309,30 @@ def tile_waveletmultiheadattention_kernel(
             quantise_x(pair)
             if pair == 0:
                 for t in range(2):
-                    spread_bias(beta_qk[:, t, :], [(w, t, ones) for w in QK])
+                    spread_bias(beta_qk[:, t, :], [(w, t, ones) for w in QK], t)
+            if pair == 1:
+                spread_bias(beta_v[:, 0, :], [(2, 0, ones), (2, 1, ones)], 0)
+                spread_bias(beta_v[:, 1, :], [(2, 0, ones), (2, 1, minus_ones)], 1)
         for n in range(2):
             product(n)
             first_read(n)
         product(2)
-        spread_bias(beta_v[:, 0, :], [(2, 0, ones), (2, 1, ones)])
-        spread_bias(beta_v[:, 1, :], [(2, 0, ones), (2, 1, minus_ones)])
+        product(3)
 
         for s in range(N_TILES):
             exp_shifted(1, s)
-            product(s + 3)
+            product(s + 4)
             first_read(s + 2)
             finish_first(s - 1)
 
         for s in range(N_TILES):
+            first_read(N_TILES + s + 2)
             finish_first(s + N_TILES - 1)
             v_odd(s)
             exp_shifted(2, s)
-            product(N_TILES + s + 3)
-            first_read(N_TILES + s + 2)
-            finish_second(s - 1)
+            product(N_TILES + s + 4)
+            finish_second(s - 2)
 
         for s in range(N_TILES):
             inverse_haar(s)
-            finish_second(s + N_TILES - 1)
+            finish_second(s + N_TILES - 2)

@@ -130,7 +130,7 @@ def tile_waveletmultiheadattention_kernel(
                             x_words[:, 256 * g + u : 256 * (g + 1) : 2],
                             ident[:],
                         )
-                copy = (nc.scalar.copy, nc.vector.tensor_copy)[a]
+                copy = (nc.vector.tensor_copy, nc.scalar.copy)[a]
                 copy(
                     out=grouped[:, a, :].bitcast(F32).rearrange("p (g r u) -> p g r u", g=GROUPS, u=2),
                     in_=turned[:].rearrange("p (g u r) -> p g r u", g=GROUPS, u=2),
@@ -326,9 +326,9 @@ def tile_waveletmultiheadattention_kernel(
             finish_first(s - 1)
 
         for s in range(N_TILES):
-            first_read(N_TILES + s + 2)
             finish_first(s + N_TILES - 1)
             v_odd(s)
+            first_read(N_TILES + s + 2)
             exp_shifted(2, s)
             product(N_TILES + s + 4)
             finish_second(s - 2)

@@ -307,12 +307,10 @@ def tile_waveletmultiheadattention_kernel(
         for pair in range(X_PAIRS):
             turn_x(pair)
             quantise_x(pair)
-            if pair == 0:
-                for t in range(2):
-                    spread_bias(beta_qk[:, t, :], [(w, t, ones) for w in QK], t)
-            if pair == 1:
-                spread_bias(beta_v[:, 0, :], [(2, 0, ones), (2, 1, ones)], 0)
-                spread_bias(beta_v[:, 1, :], [(2, 0, ones), (2, 1, minus_ones)], 1)
+        for t in range(2):
+            spread_bias(beta_qk[:, t, :], [(w, t, ones) for w in QK], t)
+        spread_bias(beta_v[:, 0, :], [(2, 0, ones), (2, 1, ones)], 0)
+        spread_bias(beta_v[:, 1, :], [(2, 0, ones), (2, 1, minus_ones)], 1)
         for n in range(2):
             product(n)
             first_read(n)

@@ -26,6 +26,7 @@ PAIRS = E // 2
 BANK_PAIRS = BANK // 2
 X_PAIRS = N_TILES // 2
 INV_SQRT2 = 0.7071067811865476
+AHEAD = 3
 
 FLOPS = 3 * 2 * TOKENS * D * E
 
@@ -144,9 +145,9 @@ def tile_waveletmultiheadattention_kernel(
                 in_=held["grouped", pair][:].rearrange("p a c -> p (a c)"),
             )
 
-        def project(i, name, weights):
+        def project(i, name, weights, banks=(0, 1)):
             passes = [(w, g) for w in weights for g in range(GROUPS)]
-            for h in range(BANKS):
+            for h in banks:
                 acc = psum_acc.tile([P, BANK], F32, tag="acc%d" % h)
                 for n, (w, g) in enumerate(passes):
                     nc.tensor.matmul_mx(
@@ -164,9 +165,11 @@ def tile_waveletmultiheadattention_kernel(
             one = acc[:].rearrange("p (j t) -> p t j", t=2)[:, t, :]
             return one.unsqueeze(1).to_broadcast([P, 2, BANK_PAIRS])
 
-        def qk_out_of_psum(i):
-            biased = work.tile([P, 2, PAIRS], F32, tag="biased")
-            for h in range(BANKS):
+        def qk_out_of_psum(i, banks=(0, 1)):
+            if banks[0] == 0:
+                held["biased", i] = work.tile([P, 2, PAIRS], F32, tag="biased", name="biased")
+            biased = held["biased", i]
+            for h in banks:
                 cols = slice(h * BANK_PAIRS, (h + 1) * BANK_PAIRS)
                 nc.vector.scalar_tensor_tensor(
                     out=biased[:, :, cols],
@@ -176,18 +179,18 @@ def tile_waveletmultiheadattention_kernel(
                     op0=ALU.mult,
                     op1=ALU.add,
                 )
-            held["biased", i] = biased
 
-        def qk_haar(i):
+        def qk_haar(i, cols=slice(0, PAIRS)):
             biased = held["biased", i]
-            bands = whole.tile([P, 2, PAIRS], F32, tag="bands")
+            if cols.start == 0:
+                held["bands", i] = whole.tile([P, 2, PAIRS], F32, tag="bands", name="bands")
+            bands = held["bands", i]
             nc.gpsimd.tensor_tensor(
-                out=bands[:, 0, :], in0=biased[:, 0, :], in1=biased[:, 1, :], op=ALU.add
+                out=bands[:, 0, cols], in0=biased[:, 0, cols], in1=biased[:, 1, cols], op=ALU.add
             )
             nc.gpsimd.tensor_tensor(
-                out=bands[:, 1, :], in0=biased[:, 1, :], in1=biased[:, 0, :], op=ALU.subtract
+                out=bands[:, 1, cols], in0=biased[:, 1, cols], in1=biased[:, 0, cols], op=ALU.subtract
             )
-            held["bands", i] = bands
 
         def exp_shifted(stage, i):
             bands = held["bands", i]
@@ -311,24 +314,26 @@ def tile_waveletmultiheadattention_kernel(
             spread_bias(beta_qk[:, t, :], [(w, t, ones) for w in QK], t)
         spread_bias(beta_v[:, 0, :], [(2, 0, ones), (2, 1, ones)], 0)
         spread_bias(beta_v[:, 1, :], [(2, 0, ones), (2, 1, minus_ones)], 1)
-        for n in range(2):
-            product(n)
-            first_read(n)
-        product(2)
-        product(3)
+        for h in range(BANKS):
+            for i in range(AHEAD):
+                project(i, "qk", QK, (h,))
+            for i in range(AHEAD):
+                qk_out_of_psum(i, (h,))
+                qk_haar(i, slice(h * BANK_PAIRS, (h + 1) * BANK_PAIRS))
+        product(AHEAD)
 
         for s in range(N_TILES):
             exp_shifted(1, s)
-            product(s + 4)
-            first_read(s + 2)
+            product(s + AHEAD + 1)
+            first_read(s + AHEAD)
             finish_first(s - 1)
 
         for s in range(N_TILES):
             finish_first(s + N_TILES - 1)
             v_odd(s)
-            first_read(N_TILES + s + 2)
+            product(N_TILES + s + AHEAD + 1)
+            first_read(N_TILES + s + AHEAD)
             exp_shifted(2, s)
-            product(N_TILES + s + 4)
             finish_second(s - 2)
 
         for s in range(N_TILES):

@@ -26,6 +26,7 @@ PAIRS = E // 2
 BANK_PAIRS = BANK // 2
 X_PAIRS = N_TILES // 2
 INV_SQRT2 = 0.7071067811865476
+G_TILES = 2
 AHEAD = 3
 
 FLOPS = 3 * 2 * TOKENS * D * E
@@ -280,6 +281,13 @@ def tile_waveletmultiheadattention_kernel(
                 )
             held["gains", i] = gains
             held["high", i] = high
+            if i < G_TILES:
+                nc.scalar.activation(
+                    out=held["bands", i][:, 0, :],
+                    in_=held["bands", i][:, 0, :],
+                    func=ACT.Copy,
+                    scale=gains[:, 0:1],
+                )
 
         def inverse_haar(i):
             rows = whole.tile([P, E], F32, tag="rows")
@@ -290,6 +298,16 @@ def tile_waveletmultiheadattention_kernel(
                 in1=held["high", i][:].rearrange("p t j -> p j t"),
                 op0=ALU.mult,
                 op1=ALU.add,
+            )
+            nc.sync.dma_start(out=out_tiles[:, i, :], in_=rows[:])
+
+        def inverse_haar_gpsimd(i):
+            rows = whole.tile([P, E], F32, tag="rows")
+            nc.gpsimd.tensor_tensor(
+                out=rows[:].rearrange("p (j t) -> p j t", t=2),
+                in0=held["bands", i][:, 0, :].unsqueeze(2).to_broadcast([P, PAIRS, 2]),
+                in1=held["high", i][:].rearrange("p t j -> p j t"),
+                op=ALU.add,
             )
             nc.sync.dma_start(out=out_tiles[:, i, :], in_=rows[:])
 
@@ -334,8 +352,11 @@ def tile_waveletmultiheadattention_kernel(
             product(N_TILES + s + AHEAD + 1)
             first_read(N_TILES + s + AHEAD)
             exp_shifted(2, s)
-            finish_second(s - 2)
+            finish_second(s - 1)
+            if 0 <= s - (N_TILES - AHEAD) < G_TILES:
+                inverse_haar_gpsimd(s - (N_TILES - AHEAD))
 
-        for s in range(N_TILES):
+        for s in range(G_TILES, N_TILES):
             inverse_haar(s)
-            finish_second(s + N_TILES - 2)
+            if s == G_TILES + 1:
+                finish_second(N_TILES - 1)

from contextlib import ExitStack

import concourse.mybir as mybir
from concourse.masks import make_identity

F32 = mybir.dt.float32
BF16 = mybir.dt.bfloat16
I32 = mybir.dt.int32
U32 = mybir.dt.uint32
U8 = mybir.dt.uint8
FP8X4 = mybir.dt.float8_e4m3fn_x4
ALU = mybir.AluOpType
ACT = mybir.ActivationFunctionType
AXIS = mybir.AxisListType

P = 128
TOKENS = 1024
D = 1024
E = 1024
N_TILES = TOKENS // P
K_PASS = 512
GROUPS = D // K_PASS
BANK = 512
BANKS = E // BANK
PAIRS = E // 2
BANK_PAIRS = BANK // 2
X_PAIRS = N_TILES // 2
INV_SQRT2 = 0.7071067811865476
G_TILES = 2
AHEAD = 3

FLOPS = 3 * 2 * TOKENS * D * E


def tile_waveletmultiheadattention_kernel(
    tc, x, W_q_words, W_q_scales, b_q, W_k_words, W_k_scales, b_k, W_v_words, W_v_scales, b_v, out
):
    nc = tc.nc
    x_tiles = x.flatten_outer_dims().rearrange("(p i) k -> p i k", i=N_TILES)
    out_tiles = out.flatten_outer_dims().rearrange("(p i) n -> p i n", i=N_TILES)
    words_in = (W_q_words, W_k_words, W_v_words)
    scales_in = (W_q_scales, W_k_scales, W_v_scales)
    biases_in = (b_q, b_k, b_v)
    QK = (0, 1)
    V = (2,)

    with ExitStack() as ctx:
        keep = ctx.enter_context(tc.tile_pool(name="keep", bufs=1))
        work = ctx.enter_context(tc.tile_pool(name="work", bufs=3))
        whole = ctx.enter_context(tc.tile_pool(name="whole", bufs=N_TILES))
        stats = ctx.enter_context(tc.tile_pool(name="stats", bufs=4))
        psum_acc = ctx.enter_context(tc.psum_pool(name="psum_acc", bufs=4))
        ctx.enter_context(tc.manual_schedule())

        x_sb = keep.tile([P, N_TILES, D], BF16)
        x_codes = keep.tile([P, N_TILES, GROUPS * P], U32, align_bytes=64)
        x_planes = keep.tile([P, N_TILES, GROUPS * P], U8, align_bytes=64)
        w_words = keep.tile([P, 3, GROUPS, E], U32, align_bytes=64)
        w_planes = keep.tile([P, 3, E], U8, align_bytes=64)
        bias_rows = keep.tile([P, 3, E], BF16)
        beta_qk = keep.tile([P, 2, PAIRS], F32)
        beta_v = keep.tile([P, 2, PAIRS], F32)
        ident = keep.tile([P, P], F32)
        ones = keep.tile([P, P], BF16)
        minus_ones = keep.tile([P, P], BF16)
        warm = keep.tile([P, 1], F32)

        nc.vector.memset(bias_rows[:].rearrange("p w n -> p (w n)").bitcast(I32), 0)
        nc.vector.memset(w_planes[:].rearrange("p w n -> p (w n)").bitcast(I32), 0)
        nc.vector.memset(ones[:], 1.0)
        nc.vector.memset(minus_ones[:], -1.0)
        nc.vector.memset(warm[:], 0.0)
        make_identity(nc, ident[:])

        def load_x(pair):
            nc.sync.dma_start(
                out=x_sb[:, 2 * pair : 2 * pair + 2, :], in_=x_tiles[:, 2 * pair : 2 * pair + 2, :]
            )

        def load_words(w, h):
            src = words_in[w].rearrange("g p n t -> p g (n t)")
            nc.sync.dma_start(
                out=w_words[:, w, :, h * BANK : (h + 1) * BANK].bitcast(I32),
                in_=src[:, :, 4 * h * BANK : 4 * (h + 1) * BANK].bitcast(I32),
            )

        def load_planes(w):
            for c in range(4):
                nc.sync.dma_start(
                    out=w_planes[32 * c : 32 * c + 4 * GROUPS, w, :].bitcast(I32),
                    in_=scales_in[w][:, 4 * c : 4 * c + 4, :].bitcast(I32),
                )

        for w in range(3):
            nc.scalar.dma_start(
                out=bias_rows[0:1, w, :], in_=biases_in[w].rearrange("(o n) -> o n", o=1)
            )
        nc.scalar.activation(out=warm[:], in_=warm[:], func=ACT.Exp)
        for pair in range(X_PAIRS):
            load_x(pair)
        for h, w_planes_now in enumerate(QK):
            load_planes(w_planes_now)
            for w in QK:
                load_words(w, h)
        load_planes(2)
        for h in range(BANKS):
            load_words(2, h)

        held = {}

        def spread_bias(plane, terms, h):
            spread = psum_acc.tile([P, BANK], F32, tag="acc%d" % h)
            for n, (w, t, sign) in enumerate(terms):
                nc.tensor.matmul(
                    out=spread[:],
                    lhsT=sign[:],
                    rhs=bias_rows[:, w, t:E:2],
                    start=(n == 0),
                    stop=(n == len(terms) - 1),
                )
            nc.scalar.activation(out=plane, in_=spread[:], func=ACT.Copy, scale=INV_SQRT2)

        def turn_x(pair):
            grouped = work.tile([P, 2, GROUPS * P * 4], BF16, align_bytes=64, tag="grouped", bufs=2)
            for a in range(2):
                x_words = x_sb[:, 2 * pair + a, :].bitcast(F32)
                turned = psum_acc.tile([P, BANK], F32, tag="acc%d" % a)
                for g in range(GROUPS):
                    for u in range(2):
                        nc.tensor.transpose(
                            turned[:, (2 * g + u) * P : (2 * g + u + 1) * P],
                            x_words[:, 256 * g + u : 256 * (g + 1) : 2],
                            ident[:],
                        )
                copy = (nc.vector.tensor_copy, nc.scalar.copy)[a]
                copy(
                    out=grouped[:, a, :].bitcast(F32).rearrange("p (g r u) -> p g r u", g=GROUPS, u=2),
                    in_=turned[:].rearrange("p (g u r) -> p g r u", g=GROUPS, u=2),
                )
            held["grouped", pair] = grouped

        def quantise_x(pair):
            nc.vector.quantize_mx(
                out=x_codes[:, 2 * pair : 2 * pair + 2, :].rearrange("p a c -> p (a c)").bitcast(FP8X4),
                scales=x_planes[:, 2 * pair : 2 * pair + 2, :].rearrange("p a c -> p (a c)"),
                in_=held["grouped", pair][:].rearrange("p a c -> p (a c)"),
            )

        def project(i, name, weights, banks=(0, 1)):
            passes = [(w, g) for w in weights for g in range(GROUPS)]
            for h in banks:
                acc = psum_acc.tile([P, BANK], F32, tag="acc%d" % h)
                for n, (w, g) in enumerate(passes):
                    nc.tensor.matmul_mx(
                        out=acc[:],
                        lhsT=x_codes[:, i, g * P : (g + 1) * P].bitcast(FP8X4),
                        lhsT_scale=x_planes[:, i, g * P : (g + 1) * P],
                        rhs=w_words[:, w, g, h * BANK : (h + 1) * BANK].bitcast(FP8X4),
                        rhs_scale=w_planes[4 * g : P, w, h * BANK : (h + 1) * BANK],
                        start=(n == 0),
                        stop=(n == len(passes) - 1),
                    )
                held[name, h, i] = acc

        def parity(acc, t):
            one = acc[:].rearrange("p (j t) -> p t j", t=2)[:, t, :]
            return one.unsqueeze(1).to_broadcast([P, 2, BANK_PAIRS])

        def qk_out_of_psum(i, banks=(0, 1)):
            if banks[0] == 0:
                held["biased", i] = work.tile([P, 2, PAIRS], F32, tag="biased", name="biased")
            biased = held["biased", i]
            for h in banks:
                cols = slice(h * BANK_PAIRS, (h + 1) * BANK_PAIRS)
                nc.vector.scalar_tensor_tensor(
                    out=biased[:, :, cols],
                    in0=held["qk", h, i][:].rearrange("p (j t) -> p t j", t=2),
                    scalar=INV_SQRT2,
                    in1=beta_qk[:, :, cols],
                    op0=ALU.mult,
                    op1=ALU.add,
                )

        def qk_haar(i, cols=slice(0, PAIRS)):
            biased = held["biased", i]
            if cols.start == 0:
                held["bands", i] = whole.tile([P, 2, PAIRS], F32, tag="bands", name="bands")
            bands = held["bands", i]
            nc.gpsimd.tensor_tensor(
                out=bands[:, 0, cols], in0=biased[:, 0, cols], in1=biased[:, 1, cols], op=ALU.add
            )
            nc.gpsimd.tensor_tensor(
                out=bands[:, 1, cols], in0=biased[:, 1, cols], in1=biased[:, 0, cols], op=ALU.subtract
            )

        def exp_shifted(stage, i):
            bands = held["bands", i]
            neg_max = stats.tile([P, 2], F32, tag="neg_max")
            nc.vector.tensor_reduce(
                out=neg_max[:], in_=bands[:], axis=AXIS.X, op=ALU.max, negate=True
            )
            total = stats.tile([P, 2], F32, tag="total")
            for band in range(2):
                nc.scalar.activation(
                    out=bands[:, band, :],
                    in_=bands[:, band, :],
                    func=ACT.Exp,
                    bias=neg_max[:, band : band + 1],
                    scale=1.0,
                    accum_out=total[:, band : band + 1],
                )
            held["total", stage, i] = total

        def live(i):
            return 0 <= i < N_TILES

        def finish_first(i):
            if not live(i):
                return
            inv = stats.tile([P, 2], F32, tag="inv")
            nc.vector.reciprocal(out=inv[:], in_=held["total", 1, i][:])
            bands = held["bands", i]
            for band in range(2):
                nc.scalar.activation(
                    out=bands[:, band, :],
                    in_=bands[:, band, :],
                    func=ACT.Copy,
                    scale=inv[:, band : band + 1],
                )

        def v_even(i):
            part = work.tile([P, 2, PAIRS], F32, tag="part")
            for h in range(BANKS):
                cols = slice(h * BANK_PAIRS, (h + 1) * BANK_PAIRS)
                nc.vector.scalar_tensor_tensor(
                    out=part[:, :, cols],
                    in0=parity(held["v", h, i], 0),
                    scalar=INV_SQRT2,
                    in1=beta_v[:, :, cols],
                    op0=ALU.mult,
                    op1=ALU.add,
                )
            held["part", i] = part

        def add_part(i):
            bands = held["bands", i]
            for band, op in enumerate((ALU.add, ALU.subtract)):
                nc.gpsimd.tensor_tensor(
                    out=bands[:, band, :],
                    in0=bands[:, band, :],
                    in1=held["part", i][:, band, :],
                    op=op,
                )

        def v_odd(i):
            bands = held["bands", i]
            for h in range(BANKS):
                cols = slice(h * BANK_PAIRS, (h + 1) * BANK_PAIRS)
                nc.vector.scalar_tensor_tensor(
                    out=bands[:, :, cols],
                    in0=parity(held["v", h, i], 1),
                    scalar=INV_SQRT2,
                    in1=bands[:, :, cols],
                    op0=ALU.mult,
                    op1=ALU.add,
                )

        def finish_second(i):
            if not live(i):
                return
            inv = stats.tile([P, 2], F32, tag="inv")
            nc.vector.reciprocal(out=inv[:], in_=held["total", 2, i][:])
            gains = whole.tile([P, 2], F32, tag="gains")
            nc.scalar.activation(out=gains[:], in_=inv[:], func=ACT.Copy, scale=INV_SQRT2)
            minus = stats.tile([P, 1], F32, tag="minus")
            nc.scalar.activation(out=minus[:], in_=inv[:, 1:2], func=ACT.Copy, scale=-INV_SQRT2)
            high = whole.tile([P, 2, PAIRS], F32, tag="high")
            for t, gain in enumerate((minus[:], gains[:, 1:2])):
                nc.scalar.activation(
                    out=high[:, t, :], in_=held["bands", i][:, 1, :], func=ACT.Copy, scale=gain
                )
            held["gains", i] = gains
            held["high", i] = high
            if i < G_TILES:
                nc.scalar.activation(
                    out=held["bands", i][:, 0, :],
                    in_=held["bands", i][:, 0, :],
                    func=ACT.Copy,
                    scale=gains[:, 0:1],
                )

        def inverse_haar(i):
            rows = whole.tile([P, E], F32, tag="rows")
            nc.vector.scalar_tensor_tensor(
                out=rows[:].rearrange("p (j t) -> p j t", t=2),
                in0=held["bands", i][:, 0, :].unsqueeze(2).to_broadcast([P, PAIRS, 2]),
                scalar=held["gains", i][:, 0:1],
                in1=held["high", i][:].rearrange("p t j -> p j t"),
                op0=ALU.mult,
                op1=ALU.add,
            )
            nc.sync.dma_start(out=out_tiles[:, i, :], in_=rows[:])

        def inverse_haar_gpsimd(i):
            rows = whole.tile([P, E], F32, tag="rows")
            nc.gpsimd.tensor_tensor(
                out=rows[:].rearrange("p (j t) -> p j t", t=2),
                in0=held["bands", i][:, 0, :].unsqueeze(2).to_broadcast([P, PAIRS, 2]),
                in1=held["high", i][:].rearrange("p t j -> p j t"),
                op=ALU.add,
            )
            nc.sync.dma_start(out=out_tiles[:, i, :], in_=rows[:])

        def product(n):
            if n < N_TILES:
                project(n, "qk", QK)
            elif n < 2 * N_TILES:
                project(n - N_TILES, "v", V)

        def first_read(n):
            if n < N_TILES:
                qk_out_of_psum(n)
                qk_haar(n)
            elif n < 2 * N_TILES:
                v_even(n - N_TILES)
                add_part(n - N_TILES)

        for pair in range(X_PAIRS):
            turn_x(pair)
            quantise_x(pair)
        for t in range(2):
            spread_bias(beta_qk[:, t, :], [(w, t, ones) for w in QK], t)
        spread_bias(beta_v[:, 0, :], [(2, 0, ones), (2, 1, ones)], 0)
        spread_bias(beta_v[:, 1, :], [(2, 0, ones), (2, 1, minus_ones)], 1)
        for h in range(BANKS):
            for i in range(AHEAD):
                project(i, "qk", QK, (h,))
            for i in range(AHEAD):
                qk_out_of_psum(i, (h,))
                qk_haar(i, slice(h * BANK_PAIRS, (h + 1) * BANK_PAIRS))
        product(AHEAD)

        for s in range(N_TILES):
            exp_shifted(1, s)
            product(s + AHEAD + 1)
            first_read(s + AHEAD)
            finish_first(s - 1)

        for s in range(N_TILES):
            finish_first(s + N_TILES - 1)
            v_odd(s)
            product(N_TILES + s + AHEAD + 1)
            first_read(N_TILES + s + AHEAD)
            exp_shifted(2, s)
            finish_second(s - 1)
            if 0 <= s - (N_TILES - AHEAD) < G_TILES:
                inverse_haar_gpsimd(s - (N_TILES - AHEAD))

        for s in range(G_TILES, N_TILES):
            inverse_haar(s)
            if s == G_TILES + 1:
                finish_second(N_TILES - 1)
